import numpy as np
import ml_dtypes


def mxq(x, axis, fmt="e4m3"):
    dtype, down = {"e4m3": (ml_dtypes.float8_e4m3fn, 7), "e5m2": (ml_dtypes.float8_e5m2, 14)}[fmt]
    v = np.moveaxis(np.asarray(x, np.float32).astype(ml_dtypes.bfloat16).astype(np.float64), axis, -1)
    blocks = v.reshape(v.shape[:-1] + (-1, 32))
    amax = np.abs(blocks).max(-1, keepdims=True)
    byte = np.maximum(np.where(amax > 0, np.frexp(amax)[1] - 1 + 127, 0) - down, 1)
    scale = np.exp2(byte - 127.0)
    codes = (blocks / scale).astype(np.float32).astype(dtype).astype(np.float64)
    return np.moveaxis((codes * scale).reshape(v.shape), -1, axis)


WIDE = False


def mx_kscale(k):
    if not WIDE:
        return np.ones(k)
    levels = np.array([10, -10, 5, -5, 0])
    a = np.random.permutation(np.resize(levels, k // 512 * 4)).reshape(k // 512, 4)
    idx = np.arange(k)
    return np.exp2(a[idx // 512, idx % 128 // 32])


BF16 = ml_dtypes.bfloat16


def bf(x):
    return np.asarray(x, np.float32).astype(BF16)


def f64(x):
    return np.asarray(x).astype(np.float64)


E2M1 = np.array([0.0, 0.5, 1.0, 1.5, 2.0, 3.0, 4.0, 6.0, -0.0, -0.5, -1.0, -1.5, -2.0, -3.0, -4.0, -6.0])


def pack_weight(w, fmt):
    k, n = w.shape
    w = f64(bf(w)).reshape(k // 32, 32, n)
    amax = np.abs(w).max(1)
    if fmt == "e4m3":
        byte = np.frexp(amax)[1] - 1 + 127 - 7
    else:
        mant, ex = np.frexp(amax / 6.0)
        byte = np.where(mant > 0.5, ex, ex - 1) + 127
    byte = np.clip(np.where(amax > 0, byte, 1), 1, 254)
    scaled = (w * np.exp2(127.0 - byte)[:, None, :]).reshape(k, n).astype(np.float32)
    by_word = np.ascontiguousarray(scaled.reshape(k // 512, 128, 4, n).transpose(0, 1, 3, 2))
    if fmt == "e4m3":
        words = by_word.astype(ml_dtypes.float8_e4m3fn).view(np.uint8)
    else:
        c = by_word.astype(ml_dtypes.float4_e2m1fn).view(np.uint8) & 0xF
        words = c[..., 0::2] | (c[..., 1::2] << 4)
    return np.ascontiguousarray(words), np.ascontiguousarray(byte.astype(np.uint8).reshape(k // 512, 16, n))


def unpack_weight(words, scales, fmt):
    g, p, n, _ = words.shape
    if fmt == "e4m3":
        vals = np.ascontiguousarray(words).view(ml_dtypes.float8_e4m3fn).astype(np.float64)
    else:
        nib = np.empty((g, p, n, 4), np.uint8)
        nib[..., 0::2] = words & 0xF
        nib[..., 1::2] = words >> 4
        vals = E2M1[nib]
    vals = vals * np.repeat(np.exp2(scales.astype(np.float64) - 127.0), 8, axis=1)[..., None]
    return vals.transpose(0, 1, 3, 2).reshape(g * 512, n)


B, C, H, W = 2, 2048, 8, 8
OFFSETS = [(-1, 0), (1, 0), (0, -1), (0, 1), (-1, -1), (-1, 1), (1, -1), (1, 1)]


def _neighbor_mean(x):
    p = np.pad(x, ((0, 0), (0, 0), (1, 1), (1, 1)), mode="edge")
    h, w = x.shape[2], x.shape[3]
    s = None
    for dy, dx in OFFSETS:
        sl = p[:, :, 1 + dy:1 + dy + h, 1 + dx:1 + dx + w]
        s = sl if s is None else s + sl
    return s / 8.0


def setup_inputs():
    s = mx_kscale(C)
    s = s / s.max()
    x = bf(np.random.standard_normal((B, C, H, W)) * s[None, :, None, None])
    wp = np.random.standard_normal((C, 2 * C)) / np.sqrt(C) / np.concatenate([s, s])[None, :]
    words, scales = pack_weight(np.ascontiguousarray(wp.T), "e4m3")
    b = bf(np.random.standard_normal(C) * 0.3)
    return {"x": x, "Wp_words": words, "Wp_scales": scales, "b": b}


def reference(x, Wp_words, Wp_scales, b):
    x, b = f64(x), f64(b)
    wt = unpack_weight(Wp_words, Wp_scales, "e4m3")
    n, c, h, w = x.shape
    mean = _neighbor_mean(x)
    xq = mxq(x, 1, "e4m3").reshape(n, c, h * w)
    mq = mxq(mean, 1, "e4m3").reshape(n, c, h * w)
    out = ((wt[:c].T @ xq)
           + (wt[c:].T @ mq)).reshape(n, c, h, w) + b[None, :, None, None]
    return np.maximum(out, 0.0) + x

@@ -1,0 +1,200 @@
+from contextlib import ExitStack
+
+import concourse.bass as bass
+import concourse.mybir as mybir
+import concourse.tile as tile
+from concourse.masks import make_identity
+
+BF16 = mybir.dt.bfloat16
+F32 = mybir.dt.float32
+I32 = mybir.dt.int32
+U8 = mybir.dt.uint8
+U32 = mybir.dt.uint32
+FP8X4 = mybir.dt.float8_e4m3fn_x4
+ALU = mybir.AluOpType
+
+P = 128
+NB = 2
+C = 2048
+S = 64
+TOK = NB * S
+GX = 4
+G = 2 * GX
+NQ = 4
+OQ = 512
+GA = 6
+
+FLOPS = 2 * TOK * 2 * C * C
+
+
+def tile_staticgraphmodule_w_kernel(tc, x, Wp_words, Wp_scales, b, out):
+    nc = tc.nc
+    with ExitStack() as ctx:
+        keep = ctx.enter_context(tc.tile_pool(name="keep", bufs=1))
+        psum = ctx.enter_context(tc.psum_pool(name="psum", bufs=1))
+        ctx.enter_context(tc.manual_schedule())
+
+        raw = keep.tile([P, NB, GX, 4 * S], BF16, align_bytes=64)
+        nc.sync.dma_start(
+            out=raw[:].rearrange("p n g f -> p (n g) f"),
+            in_=x.rearrange("n (g p t) h w -> p (n g) (t h w)", g=GX, p=P, t=4),
+        )
+        planes = [keep.tile([P, C], U8, align_bytes=64, name="plane%d" % a) for a in range(2)]
+        for a in range(2):
+            nc.vector.memset(planes[a][:].bitcast(I32), 0)
+            for q in range(4):
+                nc.sync.dma_start(
+                    out=planes[a][32 * q : 32 * q + 16, :].bitcast(I32),
+                    in_=Wp_scales[4 * a : 4 * a + 4, 4 * q : 4 * q + 4, :].bitcast(I32),
+                )
+        wts = []
+        for g in range(GA):
+            wt = keep.tile([P, 4 * C], U8, align_bytes=64, name="wt%d" % g)
+            nc.sync.dma_start(
+                out=wt[:].bitcast(I32),
+                in_=Wp_words[g].rearrange("p n t -> p (n t)").bitcast(I32),
+            )
+            wts.append(wt)
+        wlast = []
+        for q in range(NQ):
+            wq = keep.tile([P, G - GA, 4 * OQ], U8, align_bytes=64, name="wq%d" % q)
+            nc.sync.dma_start(
+                out=wq[:].bitcast(I32),
+                in_=Wp_words[GA:G, :, OQ * q : OQ * (q + 1), :].rearrange("g p n t -> p g (n t)").bitcast(I32),
+            )
+            wlast.append(wq)
+
+        ident_b = keep.tile([P, P], BF16)
+        ident_f = keep.tile([P, P], F32)
+        make_identity(nc, ident_b[:])
+        make_identity(nc, ident_f[:])
+        brow = keep.tile([P, C], BF16)
+        ones = keep.tile([P, P], BF16)
+        nc.vector.memset(brow[:].bitcast(I32), 0)
+        nc.vector.memset(ones[:], 1.0)
+        nc.scalar.dma_start(out=brow[0:1, :], in_=b.unsqueeze(0))
+
+        hmat = keep.tile([P, 16, 8], F32)
+        i3 = ident_f[:].rearrange("p (a j) -> p a j", j=8)
+        nc.vector.tensor_tensor(out=hmat[:, :, 1:8], in0=i3[:, :, 1:8], in1=i3[:, :, 0:7], op=ALU.add)
+        nc.vector.tensor_scalar_mul(out=hmat[:, :, 0:1], in0=i3[:, :, 0:1], scalar1=2.0)
+        nc.vector.tensor_tensor(out=hmat[:, :, 0:7], in0=hmat[:, :, 0:7], in1=i3[:, :, 1:8], op=ALU.add)
+        nc.vector.tensor_tensor(out=hmat[:, :, 7:8], in0=hmat[:, :, 7:8], in1=i3[:, :, 7:8], op=ALU.add)
+        bmat = keep.tile([P, 2, 8, 8], F32)
+        h4 = hmat[:].rearrange("p (e i) j -> p e i j", e=2)
+        nc.vector.tensor_tensor(out=bmat[:, :, 1:8, :], in0=h4[:, :, 1:8, :], in1=h4[:, :, 0:7, :], op=ALU.add)
+        nc.vector.tensor_scalar_mul(out=bmat[:, :, 0:1, :], in0=h4[:, :, 0:1, :], scalar1=2.0)
+        nc.vector.tensor_tensor(out=bmat[:, :, 0:7, :], in0=bmat[:, :, 0:7, :], in1=h4[:, :, 1:8, :], op=ALU.add)
+        nc.vector.tensor_tensor(out=bmat[:, :, 7:8, :], in0=bmat[:, :, 7:8, :], in1=h4[:, :, 7:8, :], op=ALU.add)
+        bflat = bmat[:].rearrange("p e i j -> p (e i j)")
+        nc.vector.tensor_tensor(out=bflat, in0=bflat, in1=ident_f[:], op=ALU.subtract)
+        amat = keep.tile([P, P], BF16)
+        nc.vector.tensor_scalar_mul(out=amat[:], in0=bflat, scalar1=0.125)
+
+        xt_sb = keep.tile([P, GX, 4, P], BF16)
+        for g in range(GX):
+            xt_ps = psum.tile([P, 4, P], BF16, tag="bank%d" % g, name="xt_ps%d" % g)
+            for n in range(NB):
+                for u in range(2):
+                    nc.tensor.transpose(xt_ps[:, 2 * n + u, :], raw[:, n, g, P * u : P * u + P], ident_b[:])
+            nc.scalar.copy(out=xt_sb[:, g], in_=xt_ps[:])
+        grouped_x = keep.tile([P, GX, NB, S, 4], BF16, align_bytes=64)
+        for g in range(GX):
+            nc.vector.tensor_copy(
+                out=grouped_x[:, g],
+                in_=raw[:, :, g, :].rearrange("p n (t s) -> p n s t", t=4),
+            )
+        codes_x = keep.tile([P, GX * TOK], U32, align_bytes=64)
+        scales_x = keep.tile([P, GX * TOK], U8, align_bytes=64)
+        nc.vector.quantize_mx(
+            out=codes_x[:].bitcast(FP8X4),
+            scales=scales_x[:],
+            in_=grouped_x[:].rearrange("p g n s t -> p (g n s t)"),
+        )
+
+        grouped_m = keep.tile([P, GX, NB, S, 4], BF16, align_bytes=64)
+        for g in range(GX):
+            m_ps = psum.tile([P, NB, 4, S], F32, tag="bank%d" % (4 + g), name="m_ps%d" % g)
+            for n in range(NB):
+                for u in range(2):
+                    nc.tensor.matmul(
+                        out=m_ps[:, n, 2 * u : 2 * u + 2, :].rearrange("p e s -> p (e s)"),
+                        lhsT=xt_sb[:, g, 2 * n + u, :],
+                        rhs=amat[:],
+                        start=True,
+                        stop=True,
+                    )
+            src = m_ps[:].rearrange("p n t s -> p n s t")
+            if g % 2 == 0:
+                nc.vector.tensor_copy(out=grouped_m[:, g], in_=src)
+            else:
+                nc.scalar.copy(out=grouped_m[:, g], in_=src)
+        codes_m = keep.tile([P, GX * TOK], U32, align_bytes=64)
+        scales_m = keep.tile([P, GX * TOK], U8, align_bytes=64)
+        nc.vector.quantize_mx(
+            out=codes_m[:].bitcast(FP8X4),
+            scales=scales_m[:],
+            in_=grouped_m[:].rearrange("p g n s t -> p (g n s t)"),
+        )
+
+        bias_bc = keep.tile([P, NQ, 4, P], BF16)
+        for q in range(NQ):
+            b_ps = psum.tile([P, OQ], F32, tag="bank%d" % q, name="b_ps%d" % q)
+            nc.tensor.matmul(out=b_ps[:], lhsT=ones[:], rhs=brow[:, OQ * q : OQ * q + OQ], start=True, stop=True)
+            nc.scalar.copy(out=bias_bc[:, q], in_=b_ps[:].rearrange("p (m j) -> p j m", j=4))
+
+        accs = [psum.tile([P, OQ], F32, tag="bank%d" % (4 + q), name="acc%d" % q) for q in range(NQ)]
+
+        def mx_pass(g, q):
+            codes, scl = (codes_x, scales_x) if g < GX else (codes_m, scales_m)
+            cols = slice(TOK * (g % GX), TOK * (g % GX) + TOK)
+            k = 4 * (g % 4)
+            if g < GA:
+                words = wts[g][:, 4 * OQ * q : 4 * OQ * (q + 1)]
+            else:
+                words = wlast[q][:, g - GA, :]
+            nc.tensor.matmul_mx(
+                out=accs[q][:],
+                lhsT=codes[:, cols].bitcast(FP8X4),
+                lhsT_scale=scl[:, cols],
+                rhs=words.bitcast(FP8X4),
+                rhs_scale=planes[g // 4][k:P, OQ * q : OQ * (q + 1)],
+                start=(g == 0),
+                stop=(g == G - 1),
+            )
+
+        for g in range(GA):
+            for q in range(NQ):
+                mx_pass(g, q)
+
+        out_v = out.rearrange("n (q m j) h w -> q m n (j h w)", q=NQ, m=P, j=4)
+        ys = [keep.tile([P, 4, P], F32, name="y%d" % q) for q in range(NQ)]
+        fs = [psum.tile([P, 4, NB, S], F32, tag="bank%d" % q, name="f_ps%d" % q) for q in range(NQ)]
+        os_ = [keep.tile([P, NB, 4, S], F32, name="o%d" % q) for q in range(NQ)]
+
+        def close(q):
+            for g in range(GA, G):
+                mx_pass(g, q)
+            nc.vector.tensor_tensor(
+                out=ys[q][:], in0=accs[q][:].rearrange("p (m j) -> p j m", j=4), in1=bias_bc[:, q], op=ALU.add
+            )
+
+        def finish(q):
+            for j in range(4):
+                nc.tensor.transpose(fs[q][:, j].rearrange("p n s -> p (n s)"), ys[q][:, j, :], ident_f[:])
+            for n in range(NB):
+                nc.vector.scalar_tensor_tensor(
+                    out=os_[q][:, n],
+                    in0=fs[q][:, :, n, :],
+                    scalar=0.0,
+                    in1=raw[:, n, q, :].rearrange("p (j s) -> p j s", j=4),
+                    op0=ALU.max,
+                    op1=ALU.add,
+                )
+            nc.sync.dma_start(out=out_v[q], in_=os_[q][:].rearrange("p n j s -> p n (j s)"))
+
+        close(0)
+        for q in range(1, NQ):
+            close(q)
+            finish(q - 1)
+        finish(NQ - 1)

@@ -35,26 +35,34 @@ def tile_staticgraphmodule_w_kernel(tc, x, Wp_words, Wp_scales, b, out):
         ctx.enter_context(tc.manual_schedule())
 
         raw = keep.tile([P, NB, GX, 4 * S], BF16, align_bytes=64)
-        nc.sync.dma_start(
+        nc.scalar.dma_start(
             out=raw[:].rearrange("p n g f -> p (n g) f"),
             in_=x.rearrange("n (g p t) h w -> p (n g) (t h w)", g=GX, p=P, t=4),
         )
         planes = [keep.tile([P, C], U8, align_bytes=64, name="plane%d" % a) for a in range(2)]
-        for a in range(2):
-            nc.vector.memset(planes[a][:].bitcast(I32), 0)
+        wts = [keep.tile([P, 4 * C], U8, align_bytes=64, name="wt%d" % g) for g in range(GA)]
+
+        def load_scales(a):
             for q in range(4):
                 nc.sync.dma_start(
                     out=planes[a][32 * q : 32 * q + 16, :].bitcast(I32),
                     in_=Wp_scales[4 * a : 4 * a + 4, 4 * q : 4 * q + 4, :].bitcast(I32),
                 )
-        wts = []
-        for g in range(GA):
-            wt = keep.tile([P, 4 * C], U8, align_bytes=64, name="wt%d" % g)
+
+        def load_words(g):
             nc.sync.dma_start(
-                out=wt[:].bitcast(I32),
+                out=wts[g][:].bitcast(I32),
                 in_=Wp_words[g].rearrange("p n t -> p (n t)").bitcast(I32),
             )
-            wts.append(wt)
+
+        for a in range(2):
+            nc.vector.memset(planes[a][:].bitcast(I32), 0)
+        load_words(0)
+        load_scales(0)
+        load_words(1)
+        load_scales(1)
+        for g in range(2, GA):
+            load_words(g)
         wlast = []
         for q in range(NQ):
             wq = keep.tile([P, G - GA, 4 * OQ], U8, align_bytes=64, name="wq%d" % q)

@@ -145,11 +145,11 @@ def tile_staticgraphmodule_w_kernel(tc, x, Wp_words, Wp_scales, b, out):
             in_=grouped_m[:].rearrange("p g n s t -> p (g n s t)"),
         )
 
-        bias_bc = keep.tile([P, NQ, 4, P], BF16)
+        bias_bc = keep.tile([P, NQ, OQ], BF16)
         for q in range(NQ):
             b_ps = psum.tile([P, OQ], F32, tag="bank%d" % q, name="b_ps%d" % q)
             nc.tensor.matmul(out=b_ps[:], lhsT=ones[:], rhs=brow[:, OQ * q : OQ * q + OQ], start=True, stop=True)
-            nc.scalar.copy(out=bias_bc[:, q], in_=b_ps[:].rearrange("p (m j) -> p j m", j=4))
+            nc.scalar.copy(out=bias_bc[:, q], in_=b_ps[:])
 
         accs = [psum.tile([P, OQ], F32, tag="bank%d" % (4 + q), name="acc%d" % q) for q in range(NQ)]
 
@@ -184,7 +184,10 @@ def tile_staticgraphmodule_w_kernel(tc, x, Wp_words, Wp_scales, b, out):
             for g in range(GA, G):
                 mx_pass(g, q)
             nc.vector.tensor_tensor(
-                out=ys[q][:], in0=accs[q][:].rearrange("p (m j) -> p j m", j=4), in1=bias_bc[:, q], op=ALU.add
+                out=ys[q][:].rearrange("p j m -> p m j"),
+                in0=accs[q][:].rearrange("p (m j) -> p m j", j=4),
+                in1=bias_bc[:, q].rearrange("p (m j) -> p m j", j=4),
+                op=ALU.add,
             )
 
         def finish(q):

@@ -44,9 +44,9 @@ def tile_staticgraphmodule_w_kernel(tc, x, Wp_words, Wp_scales, b, out):
 
         def load_scales(a):
             for q in range(4):
-                nc.sync.dma_start(
-                    out=planes[a][32 * q : 32 * q + 16, :].bitcast(I32),
-                    in_=Wp_scales[4 * a : 4 * a + 4, 4 * q : 4 * q + 4, :].bitcast(I32),
+                nc.gpsimd.dma_start(
+                    out=planes[a][32 * q : 32 * q + 16, :].bitcast(F32),
+                    in_=Wp_scales[4 * a : 4 * a + 4, 4 * q : 4 * q + 4, :].bitcast(F32),
                 )
 
         def load_words(g):
@@ -57,11 +57,7 @@ def tile_staticgraphmodule_w_kernel(tc, x, Wp_words, Wp_scales, b, out):
 
         for a in range(2):
             nc.vector.memset(planes[a][:].bitcast(I32), 0)
-        load_words(0)
-        load_scales(0)
-        load_words(1)
-        load_scales(1)
-        for g in range(2, GA):
+        for g in range(GA):
             load_words(g)
         wlast = []
         for q in range(NQ):
@@ -76,6 +72,8 @@ def tile_staticgraphmodule_w_kernel(tc, x, Wp_words, Wp_scales, b, out):
         ident_f = keep.tile([P, P], F32)
         make_identity(nc, ident_b[:])
         make_identity(nc, ident_f[:])
+        load_scales(0)
+        load_scales(1)
         brow = keep.tile([P, C], BF16)
         ones = keep.tile([P, P], BF16)
         nc.vector.memset(brow[:].bitcast(I32), 0)
@@ -145,11 +143,11 @@ def tile_staticgraphmodule_w_kernel(tc, x, Wp_words, Wp_scales, b, out):
             in_=grouped_m[:].rearrange("p g n s t -> p (g n s t)"),
         )
 
-        bias_bc = keep.tile([P, NQ, OQ], BF16)
+        bias_bc = keep.tile([P, NQ, 4, P], BF16)
         for q in range(NQ):
             b_ps = psum.tile([P, OQ], F32, tag="bank%d" % q, name="b_ps%d" % q)
             nc.tensor.matmul(out=b_ps[:], lhsT=ones[:], rhs=brow[:, OQ * q : OQ * q + OQ], start=True, stop=True)
-            nc.scalar.copy(out=bias_bc[:, q], in_=b_ps[:])
+            nc.scalar.copy(out=bias_bc[:, q], in_=b_ps[:].rearrange("p (m j) -> p j m", j=4))
 
         accs = [psum.tile([P, OQ], F32, tag="bank%d" % (4 + q), name="acc%d" % q) for q in range(NQ)]
 
@@ -184,10 +182,7 @@ def tile_staticgraphmodule_w_kernel(tc, x, Wp_words, Wp_scales, b, out):
             for g in range(GA, G):
                 mx_pass(g, q)
             nc.vector.tensor_tensor(
-                out=ys[q][:].rearrange("p j m -> p m j"),
-                in0=accs[q][:].rearrange("p (m j) -> p m j", j=4),
-                in1=bias_bc[:, q].rearrange("p (m j) -> p m j", j=4),
-                op=ALU.add,
+                out=ys[q][:], in0=accs[q][:].rearrange("p (m j) -> p j m", j=4), in1=bias_bc[:, q], op=ALU.add
             )
 
         def finish(q):

@@ -34,11 +34,17 @@ def tile_staticgraphmodule_w_kernel(tc, x, Wp_words, Wp_scales, b, out):
         psum = ctx.enter_context(tc.psum_pool(name="psum", bufs=1))
         ctx.enter_context(tc.manual_schedule())
 
+        b0 = keep.tile([1, C], BF16)
+        nc.scalar.dma_start(out=b0[:], in_=b.unsqueeze(0))
         raw = keep.tile([P, NB, GX, 4 * S], BF16, align_bytes=64)
-        nc.scalar.dma_start(
+        nc.sync.dma_start(
             out=raw[:].rearrange("p n g f -> p (n g) f"),
             in_=x.rearrange("n (g p t) h w -> p (n g) (t h w)", g=GX, p=P, t=4),
         )
+        ones = keep.tile([P, P], BF16)
+        nc.vector.memset(ones[:], 1.0)
+        warm = keep.tile([P, 1], BF16)
+        nc.scalar.copy(out=warm[:], in_=ones[:, 0:1])
         planes = [keep.tile([P, C], U8, align_bytes=64, name="plane%d" % a) for a in range(2)]
         wts = [keep.tile([P, 4 * C], U8, align_bytes=64, name="wt%d" % g) for g in range(GA)]
 
@@ -75,10 +81,7 @@ def tile_staticgraphmodule_w_kernel(tc, x, Wp_words, Wp_scales, b, out):
         load_scales(0)
         load_scales(1)
         brow = keep.tile([P, C], BF16)
-        ones = keep.tile([P, P], BF16)
         nc.vector.memset(brow[:].bitcast(I32), 0)
-        nc.vector.memset(ones[:], 1.0)
-        nc.scalar.dma_start(out=brow[0:1, :], in_=b.unsqueeze(0))
 
         hmat = keep.tile([P, 16, 8], F32)
         i3 = ident_f[:].rearrange("p (a j) -> p a j", j=8)
@@ -117,6 +120,7 @@ def tile_staticgraphmodule_w_kernel(tc, x, Wp_words, Wp_scales, b, out):
             scales=scales_x[:],
             in_=grouped_x[:].rearrange("p g n s t -> p (g n s t)"),
         )
+        nc.vector.tensor_copy(out=brow[0:1, :], in_=b0[:])
 
         grouped_m = keep.tile([P, GX, NB, S, 4], BF16, align_bytes=64)
         for g in range(GX):
@@ -143,13 +147,7 @@ def tile_staticgraphmodule_w_kernel(tc, x, Wp_words, Wp_scales, b, out):
             in_=grouped_m[:].rearrange("p g n s t -> p (g n s t)"),
         )
 
-        bias_bc = keep.tile([P, NQ, 4, P], BF16)
-        for q in range(NQ):
-            b_ps = psum.tile([P, OQ], F32, tag="bank%d" % q, name="b_ps%d" % q)
-            nc.tensor.matmul(out=b_ps[:], lhsT=ones[:], rhs=brow[:, OQ * q : OQ * q + OQ], start=True, stop=True)
-            nc.scalar.copy(out=bias_bc[:, q], in_=b_ps[:].rearrange("p (m j) -> p j m", j=4))
-
-        accs = [psum.tile([P, OQ], F32, tag="bank%d" % (4 + q), name="acc%d" % q) for q in range(NQ)]
+        accs = [psum.tile([P, OQ], F32, tag="bank%d" % q, name="acc%d" % q) for q in range(NQ)]
 
         def mx_pass(g, q):
             codes, scl = (codes_x, scales_x) if g < GX else (codes_m, scales_m)
@@ -169,13 +167,23 @@ def tile_staticgraphmodule_w_kernel(tc, x, Wp_words, Wp_scales, b, out):
                 stop=(g == G - 1),
             )
 
-        for g in range(GA):
+        for g in range(2):
+            for q in range(NQ):
+                mx_pass(g, q)
+
+        bias_bc = keep.tile([P, NQ, 4, P], BF16)
+        for q in range(NQ):
+            b_ps = psum.tile([P, OQ], F32, tag="bank%d" % (4 + q), name="b_ps%d" % q)
+            nc.tensor.matmul(out=b_ps[:], lhsT=ones[:], rhs=brow[:, OQ * q : OQ * q + OQ], start=True, stop=True)
+            nc.scalar.copy(out=bias_bc[:, q], in_=b_ps[:].rearrange("p (m j) -> p j m", j=4))
+
+        for g in range(2, GA):
             for q in range(NQ):
                 mx_pass(g, q)
 
         out_v = out.rearrange("n (q m j) h w -> q m n (j h w)", q=NQ, m=P, j=4)
         ys = [keep.tile([P, 4, P], F32, name="y%d" % q) for q in range(NQ)]
-        fs = [psum.tile([P, 4, NB, S], F32, tag="bank%d" % q, name="f_ps%d" % q) for q in range(NQ)]
+        fs = [psum.tile([P, 4, NB, S], F32, tag="bank%d" % (4 + q), name="f_ps%d" % q) for q in range(NQ)]
         os_ = [keep.tile([P, NB, 4, S], F32, name="o%d" % q) for q in range(NQ)]
 
         def close(q):

@@ -50,9 +50,9 @@ def tile_staticgraphmodule_w_kernel(tc, x, Wp_words, Wp_scales, b, out):
 
         def load_scales(a):
             for q in range(4):
-                nc.gpsimd.dma_start(
-                    out=planes[a][32 * q : 32 * q + 16, :].bitcast(F32),
-                    in_=Wp_scales[4 * a : 4 * a + 4, 4 * q : 4 * q + 4, :].bitcast(F32),
+                nc.sync.dma_start(
+                    out=planes[a][32 * q : 32 * q + 16, :].bitcast(I32),
+                    in_=Wp_scales[4 * a : 4 * a + 4, 4 * q : 4 * q + 4, :].bitcast(I32),
                 )
 
         def load_words(g):
@@ -63,7 +63,11 @@ def tile_staticgraphmodule_w_kernel(tc, x, Wp_words, Wp_scales, b, out):
 
         for a in range(2):
             nc.vector.memset(planes[a][:].bitcast(I32), 0)
-        for g in range(GA):
+        load_scales(0)
+        for g in range(3):
+            load_words(g)
+        load_scales(1)
+        for g in range(3, GA):
             load_words(g)
         wlast = []
         for q in range(NQ):
@@ -78,8 +82,6 @@ def tile_staticgraphmodule_w_kernel(tc, x, Wp_words, Wp_scales, b, out):
         ident_f = keep.tile([P, P], F32)
         make_identity(nc, ident_b[:])
         make_identity(nc, ident_f[:])
-        load_scales(0)
-        load_scales(1)
         brow = keep.tile([P, C], BF16)
         nc.vector.memset(brow[:].bitcast(I32), 0)
 

@@ -70,13 +70,21 @@ def tile_staticgraphmodule_w_kernel(tc, x, Wp_words, Wp_scales, b, out):
         for g in range(3, GA):
             load_words(g)
         wlast = []
-        for q in range(NQ):
+        for q in range(NQ - 1):
             wq = keep.tile([P, G - GA, 4 * OQ], U8, align_bytes=64, name="wq%d" % q)
             nc.sync.dma_start(
                 out=wq[:].bitcast(I32),
                 in_=Wp_words[GA:G, :, OQ * q : OQ * (q + 1), :].rearrange("g p n t -> p g (n t)").bitcast(I32),
             )
             wlast.append(wq)
+        wend = []
+        for g in range(GA, G):
+            we = keep.tile([P, 4 * OQ], U8, align_bytes=64, name="we%d" % g)
+            nc.sync.dma_start(
+                out=we[:].bitcast(I32),
+                in_=Wp_words[g, :, OQ * (NQ - 1) : C, :].rearrange("p n t -> p (n t)").bitcast(I32),
+            )
+            wend.append(we)
 
         ident_b = keep.tile([P, P], BF16)
         ident_f = keep.tile([P, P], F32)
@@ -157,8 +165,10 @@ def tile_staticgraphmodule_w_kernel(tc, x, Wp_words, Wp_scales, b, out):
             k = 4 * (g % 4)
             if g < GA:
                 words = wts[g][:, 4 * OQ * q : 4 * OQ * (q + 1)]
-            else:
+            elif q < NQ - 1:
                 words = wlast[q][:, g - GA, :]
+            else:
+                words = wend[g - GA][:]
             nc.tensor.matmul_mx(
                 out=accs[q][:],
                 lhsT=codes[:, cols].bitcast(FP8X4),
@@ -183,34 +193,55 @@ def tile_staticgraphmodule_w_kernel(tc, x, Wp_words, Wp_scales, b, out):
             for q in range(NQ):
                 mx_pass(g, q)
 
-        out_v = out.rearrange("n (q m j) h w -> q m n (j h w)", q=NQ, m=P, j=4)
+        out_v = out.rearrange("n (q m j) h w -> q m n j (h w)", q=NQ, m=P, j=4)
         ys = [keep.tile([P, 4, P], F32, name="y%d" % q) for q in range(NQ)]
-        fs = [psum.tile([P, 4, NB, S], F32, tag="bank%d" % (4 + q), name="f_ps%d" % q) for q in range(NQ)]
         os_ = [keep.tile([P, NB, 4, S], F32, name="o%d" % q) for q in range(NQ)]
 
-        def close(q):
+        def last_passes(q):
             for g in range(GA, G):
                 mx_pass(g, q)
+
+        def add_bias(q, j0, j1):
             nc.vector.tensor_tensor(
-                out=ys[q][:], in0=accs[q][:].rearrange("p (m j) -> p j m", j=4), in1=bias_bc[:, q], op=ALU.add
+                out=ys[q][:, j0:j1, :],
+                in0=accs[q][:].rearrange("p (m j) -> p j m", j=4)[:, j0:j1, :],
+                in1=bias_bc[:, q, j0:j1, :],
+                op=ALU.add,
             )
 
-        def finish(q):
-            for j in range(4):
-                nc.tensor.transpose(fs[q][:, j].rearrange("p n s -> p (n s)"), ys[q][:, j, :], ident_f[:])
-            for n in range(NB):
-                nc.vector.scalar_tensor_tensor(
-                    out=os_[q][:, n],
-                    in0=fs[q][:, :, n, :],
-                    scalar=0.0,
-                    in1=raw[:, n, q, :].rearrange("p (j s) -> p j s", j=4),
-                    op0=ALU.max,
-                    op1=ALU.add,
-                )
-            nc.sync.dma_start(out=out_v[q], in_=os_[q][:].rearrange("p n j s -> p n (j s)"))
+        def turn_back(q, j0, j1, bank):
+            f_ps = psum.tile([P, NB, j1 - j0, S], F32, tag="bank%d" % bank, name="f_ps%d_%d" % (q, j0))
+            for j in range(j0, j1):
+                nc.tensor.transpose(f_ps[:, :, j - j0, :], ys[q][:, j, :], ident_f[:])
+            return f_ps
 
-        close(0)
-        for q in range(1, NQ):
-            close(q)
-            finish(q - 1)
-        finish(NQ - 1)
+        def relu_residual_store(q, j0, j1, f_ps):
+            nc.vector.scalar_tensor_tensor(
+                out=os_[q][:, :, j0:j1, :].rearrange("p n j s -> p n (j s)"),
+                in0=f_ps[:].rearrange("p n j s -> p n (j s)"),
+                scalar=0.0,
+                in1=raw[:, :, q, S * j0 : S * j1],
+                op0=ALU.max,
+                op1=ALU.add,
+            )
+            nc.sync.dma_start(out=out_v[q][:, :, j0:j1, :], in_=os_[q][:, :, j0:j1, :])
+
+        last_passes(0)
+        add_bias(0, 0, 4)
+        last_passes(1)
+        add_bias(1, 0, 4)
+        f0 = turn_back(0, 0, 4, 4)
+        relu_residual_store(0, 0, 4, f0)
+        last_passes(2)
+        add_bias(2, 0, 4)
+        f1 = turn_back(1, 0, 4, 5)
+        relu_residual_store(1, 0, 4, f1)
+        last_passes(3)
+        add_bias(3, 0, 2)
+        add_bias(3, 2, 4)
+        f2 = turn_back(2, 0, 4, 6)
+        relu_residual_store(2, 0, 4, f2)
+        f3a = turn_back(3, 0, 2, 7)
+        f3b = turn_back(3, 2, 4, 4)
+        relu_residual_store(3, 0, 2, f3a)
+        relu_residual_store(3, 2, 4, f3b)

@@ -34,17 +34,18 @@ def tile_staticgraphmodule_w_kernel(tc, x, Wp_words, Wp_scales, b, out):
         psum = ctx.enter_context(tc.psum_pool(name="psum", bufs=1))
         ctx.enter_context(tc.manual_schedule())
 
-        b0 = keep.tile([1, C], BF16)
-        nc.scalar.dma_start(out=b0[:], in_=b.unsqueeze(0))
+        bq = keep.tile([P, OQ], BF16)
+        nc.vector.memset(bq[:].bitcast(I32), 0)
+        nc.scalar.dma_start(out=bq[0:NQ, :], in_=b.rearrange("(q c) -> q c", q=NQ))
         raw = keep.tile([P, NB, GX, 4 * S], BF16, align_bytes=64)
         nc.sync.dma_start(
             out=raw[:].rearrange("p n g f -> p (n g) f"),
             in_=x.rearrange("n (g p t) h w -> p (n g) (t h w)", g=GX, p=P, t=4),
         )
-        ones = keep.tile([P, P], BF16)
-        nc.vector.memset(ones[:], 1.0)
+        one = keep.tile([P, 1], BF16)
+        nc.vector.memset(one[:], 1.0)
         warm = keep.tile([P, 1], BF16)
-        nc.scalar.copy(out=warm[:], in_=ones[:, 0:1])
+        nc.scalar.copy(out=warm[:], in_=one[:])
         planes = [keep.tile([P, C], U8, align_bytes=64, name="plane%d" % a) for a in range(2)]
         wts = [keep.tile([P, 4 * C], U8, align_bytes=64, name="wt%d" % g) for g in range(GA)]
 
@@ -90,8 +91,6 @@ def tile_staticgraphmodule_w_kernel(tc, x, Wp_words, Wp_scales, b, out):
         ident_f = keep.tile([P, P], F32)
         make_identity(nc, ident_b[:])
         make_identity(nc, ident_f[:])
-        brow = keep.tile([P, C], BF16)
-        nc.vector.memset(brow[:].bitcast(I32), 0)
 
         hmat = keep.tile([P, 16, 8], F32)
         i3 = ident_f[:].rearrange("p (a j) -> p a j", j=8)
@@ -130,7 +129,6 @@ def tile_staticgraphmodule_w_kernel(tc, x, Wp_words, Wp_scales, b, out):
             scales=scales_x[:],
             in_=grouped_x[:].rearrange("p g n s t -> p (g n s t)"),
         )
-        nc.vector.tensor_copy(out=brow[0:1, :], in_=b0[:])
 
         grouped_m = keep.tile([P, GX, NB, S, 4], BF16, align_bytes=64)
         for g in range(GX):
@@ -183,11 +181,21 @@ def tile_staticgraphmodule_w_kernel(tc, x, Wp_words, Wp_scales, b, out):
             for q in range(NQ):
                 mx_pass(g, q)
 
-        bias_bc = keep.tile([P, NQ, 4, P], BF16)
+        bc_ps = psum.tile([P, 4, NQ], F32, tag="bank4", name="bc_ps")
+        for j in range(4):
+            nc.tensor.matmul(out=bc_ps[:, j, :], lhsT=bq[:, j:OQ:4], rhs=ident_b[:, 0:NQ], start=True, stop=True)
+        bcol = keep.tile([P, 4, NQ], F32)
+        nc.scalar.copy(out=bcol[:], in_=bc_ps[:])
+        nbcol = keep.tile([P, 4, NQ], F32)
+        nc.vector.tensor_scalar_mul(out=nbcol[:], in0=bcol[:], scalar1=-1.0)
+        xb = keep.tile([P, NB, NQ, 4 * S], F32)
         for q in range(NQ):
-            b_ps = psum.tile([P, OQ], F32, tag="bank%d" % (4 + q), name="b_ps%d" % q)
-            nc.tensor.matmul(out=b_ps[:], lhsT=ones[:], rhs=brow[:, OQ * q : OQ * q + OQ], start=True, stop=True)
-            nc.scalar.copy(out=bias_bc[:, q], in_=b_ps[:].rearrange("p (m j) -> p j m", j=4))
+            for j in range(4):
+                nc.vector.tensor_scalar_add(
+                    out=xb[:, :, q, S * j : S * j + S],
+                    in0=raw[:, :, q, S * j : S * j + S],
+                    scalar1=bcol[:, j, q : q + 1],
+                )
 
         for g in range(2, GA):
             for q in range(NQ):
@@ -201,13 +209,8 @@ def tile_staticgraphmodule_w_kernel(tc, x, Wp_words, Wp_scales, b, out):
             for g in range(GA, G):
                 mx_pass(g, q)
 
-        def add_bias(q, j0, j1):
-            nc.vector.tensor_tensor(
-                out=ys[q][:, j0:j1, :],
-                in0=accs[q][:].rearrange("p (m j) -> p j m", j=4)[:, j0:j1, :],
-                in1=bias_bc[:, q, j0:j1, :],
-                op=ALU.add,
-            )
+        def copy_out(q, j0, j1):
+            nc.scalar.copy(out=ys[q][:, j0:j1, :], in_=accs[q][:].rearrange("p (m j) -> p j m", j=4)[:, j0:j1, :])
 
         def turn_back(q, j0, j1, bank):
             f_ps = psum.tile([P, NB, j1 - j0, S], F32, tag="bank%d" % bank, name="f_ps%d_%d" % (q, j0))
@@ -216,29 +219,30 @@ def tile_staticgraphmodule_w_kernel(tc, x, Wp_words, Wp_scales, b, out):
             return f_ps
 
         def relu_residual_store(q, j0, j1, f_ps):
-            nc.vector.scalar_tensor_tensor(
-                out=os_[q][:, :, j0:j1, :].rearrange("p n j s -> p n (j s)"),
-                in0=f_ps[:].rearrange("p n j s -> p n (j s)"),
-                scalar=0.0,
-                in1=raw[:, :, q, S * j0 : S * j1],
-                op0=ALU.max,
-                op1=ALU.add,
-            )
+            for j in range(j0, j1):
+                nc.vector.scalar_tensor_tensor(
+                    out=os_[q][:, :, j, :],
+                    in0=f_ps[:, :, j - j0, :],
+                    scalar=nbcol[:, j, q : q + 1],
+                    in1=xb[:, :, q, S * j : S * j + S],
+                    op0=ALU.max,
+                    op1=ALU.add,
+                )
             nc.sync.dma_start(out=out_v[q][:, :, j0:j1, :], in_=os_[q][:, :, j0:j1, :])
 
         last_passes(0)
-        add_bias(0, 0, 4)
+        copy_out(0, 0, 4)
         last_passes(1)
-        add_bias(1, 0, 4)
+        copy_out(1, 0, 4)
         f0 = turn_back(0, 0, 4, 4)
         relu_residual_store(0, 0, 4, f0)
         last_passes(2)
-        add_bias(2, 0, 4)
+        copy_out(2, 0, 4)
         f1 = turn_back(1, 0, 4, 5)
         relu_residual_store(1, 0, 4, f1)
         last_passes(3)
-        add_bias(3, 0, 2)
-        add_bias(3, 2, 4)
+        copy_out(3, 0, 2)
+        copy_out(3, 2, 4)
         f2 = turn_back(2, 0, 4, 6)
         relu_residual_store(2, 0, 4, f2)
         f3a = turn_back(3, 0, 2, 7)

@@ -20,8 +20,11 @@ S = 64
 TOK = NB * S
 GX = 4
 G = 2 * GX
-NQ = 4
+NQ = 3
 OQ = 512
+CQ = NQ * OQ
+NZ = 4
+GW = 4
 GA = 6
 
 FLOPS = 2 * TOK * 2 * C * C
@@ -36,7 +39,7 @@ def tile_staticgraphmodule_w_kernel(tc, x, Wp_words, Wp_scales, b, out):
 
         bq = keep.tile([P, OQ], BF16)
         nc.vector.memset(bq[:].bitcast(I32), 0)
-        nc.scalar.dma_start(out=bq[0:NQ, :], in_=b.rearrange("(q c) -> q c", q=NQ))
+        nc.scalar.dma_start(out=bq[0:4, :], in_=b.rearrange("(q c) -> q c", q=4))
         raw = keep.tile([P, NB, GX, 4 * S], BF16, align_bytes=64)
         nc.sync.dma_start(
             out=raw[:].rearrange("p n g f -> p (n g) f"),
@@ -47,7 +50,6 @@ def tile_staticgraphmodule_w_kernel(tc, x, Wp_words, Wp_scales, b, out):
         warm = keep.tile([P, 1], BF16)
         nc.scalar.copy(out=warm[:], in_=one[:])
         planes = [keep.tile([P, C], U8, align_bytes=64, name="plane%d" % a) for a in range(2)]
-        wts = [keep.tile([P, 4 * C], U8, align_bytes=64, name="wt%d" % g) for g in range(GA)]
 
         def load_scales(a):
             for q in range(4):
@@ -56,36 +58,36 @@ def tile_staticgraphmodule_w_kernel(tc, x, Wp_words, Wp_scales, b, out):
                     in_=Wp_scales[4 * a : 4 * a + 4, 4 * q : 4 * q + 4, :].bitcast(I32),
                 )
 
-        def load_words(g):
+        words = {}
+
+        def load_words(g0, g1, c0, c1):
+            wt = keep.tile([P, g1 - g0, 4 * (c1 - c0)], U8, align_bytes=64, name="w%d_%d" % (g0, c0))
             nc.sync.dma_start(
-                out=wts[g][:].bitcast(I32),
-                in_=Wp_words[g].rearrange("p n t -> p (n t)").bitcast(I32),
+                out=wt[:].bitcast(I32),
+                in_=Wp_words[g0:g1, :, c0:c1, :].rearrange("g p n t -> p g (n t)").bitcast(I32),
             )
+            for g in range(g0, g1):
+                for c in range(c0, c1, P):
+                    if c < CQ:
+                        if c % OQ == 0:
+                            words[(g, c)] = wt[:, g - g0, 4 * (c - c0) : 4 * (c - c0 + OQ)]
+                    else:
+                        words[(g, c)] = wt[:, g - g0, 4 * (c - c0) : 4 * (c - c0 + P)]
 
         for a in range(2):
             nc.vector.memset(planes[a][:].bitcast(I32), 0)
         load_scales(0)
         for g in range(3):
-            load_words(g)
+            load_words(g, g + 1, 0, C)
         load_scales(1)
-        for g in range(3, GA):
-            load_words(g)
-        wlast = []
-        for q in range(NQ - 1):
-            wq = keep.tile([P, G - GA, 4 * OQ], U8, align_bytes=64, name="wq%d" % q)
-            nc.sync.dma_start(
-                out=wq[:].bitcast(I32),
-                in_=Wp_words[GA:G, :, OQ * q : OQ * (q + 1), :].rearrange("g p n t -> p g (n t)").bitcast(I32),
-            )
-            wlast.append(wq)
-        wend = []
-        for g in range(GA, G):
-            we = keep.tile([P, 4 * OQ], U8, align_bytes=64, name="we%d" % g)
-            nc.sync.dma_start(
-                out=we[:].bitcast(I32),
-                in_=Wp_words[g, :, OQ * (NQ - 1) : C, :].rearrange("p n t -> p (n t)").bitcast(I32),
-            )
-            wend.append(we)
+        load_words(3, 4, 0, C)
+        for g in range(GW, GA):
+            load_words(g, g + 1, 0, CQ)
+        for q in range(NQ):
+            load_words(GA, G, OQ * q, OQ * (q + 1))
+        load_words(GW, GA, CQ, C)
+        load_words(GA, GA + 1, CQ, C)
+        load_words(GA + 1, G, CQ, C)
 
         ident_b = keep.tile([P, P], BF16)
         ident_f = keep.tile([P, P], F32)
@@ -130,6 +132,11 @@ def tile_staticgraphmodule_w_kernel(tc, x, Wp_words, Wp_scales, b, out):
             in_=grouped_x[:].rearrange("p g n s t -> p (g n s t)"),
         )
 
+        spread = keep.tile([P, 4, OQ], BF16)
+        nc.vector.memset(spread[:].bitcast(I32), 0)
+        for t in range(4):
+            nc.vector.tensor_copy(out=spread[:, t, t:OQ:4], in_=ident_b[:])
+
         grouped_m = keep.tile([P, GX, NB, S, 4], BF16, align_bytes=64)
         for g in range(GX):
             m_ps = psum.tile([P, NB, 4, S], F32, tag="bank%d" % (4 + g), name="m_ps%d" % g)
@@ -156,37 +163,54 @@ def tile_staticgraphmodule_w_kernel(tc, x, Wp_words, Wp_scales, b, out):
         )
 
         accs = [psum.tile([P, OQ], F32, tag="bank%d" % q, name="acc%d" % q) for q in range(NQ)]
+        Z_BANKS = [3, 5, 6, 7]
+        z_ps = [psum.tile([P, TOK], F32, tag="bank%d" % Z_BANKS[z], name="z_ps%d" % z) for z in range(NZ)]
 
-        def mx_pass(g, q):
+        def operand(g):
             codes, scl = (codes_x, scales_x) if g < GX else (codes_m, scales_m)
             cols = slice(TOK * (g % GX), TOK * (g % GX) + TOK)
-            k = 4 * (g % 4)
-            if g < GA:
-                words = wts[g][:, 4 * OQ * q : 4 * OQ * (q + 1)]
-            elif q < NQ - 1:
-                words = wlast[q][:, g - GA, :]
-            else:
-                words = wend[g - GA][:]
+            return codes[:, cols].bitcast(FP8X4), scl[:, cols]
+
+        def quarter_pass(g, q):
+            act_codes, act_scales = operand(g)
             nc.tensor.matmul_mx(
                 out=accs[q][:],
-                lhsT=codes[:, cols].bitcast(FP8X4),
-                lhsT_scale=scl[:, cols],
-                rhs=words.bitcast(FP8X4),
-                rhs_scale=planes[g // 4][k:P, OQ * q : OQ * (q + 1)],
+                lhsT=act_codes,
+                lhsT_scale=act_scales,
+                rhs=words[(g, OQ * q)].bitcast(FP8X4),
+                rhs_scale=planes[g // 4][4 * (g % 4) : P, OQ * q : OQ * (q + 1)],
+                start=(g == 0),
+                stop=(g == G - 1),
+            )
+
+        def tile_pass(g, z):
+            act_codes, act_scales = operand(g)
+            c0 = CQ + P * z
+            nc.tensor.matmul_mx(
+                out=z_ps[z][:],
+                lhsT=words[(g, c0)].bitcast(FP8X4),
+                lhsT_scale=planes[g // 4][4 * (g % 4) : P, c0 : c0 + P],
+                rhs=act_codes,
+                rhs_scale=act_scales,
                 start=(g == 0),
                 stop=(g == G - 1),
             )
 
         for g in range(2):
             for q in range(NQ):
-                mx_pass(g, q)
+                quarter_pass(g, q)
+            tile_pass(g, 0)
 
-        bc_ps = psum.tile([P, 4, NQ], F32, tag="bank4", name="bc_ps")
+        bc_ps = psum.tile([P, 20], F32, tag="bank4", name="bc_ps")
         for j in range(4):
-            nc.tensor.matmul(out=bc_ps[:, j, :], lhsT=bq[:, j:OQ:4], rhs=ident_b[:, 0:NQ], start=True, stop=True)
-        bcol = keep.tile([P, 4, NQ], F32)
+            nc.tensor.matmul(out=bc_ps[:, 4 * j : 4 * j + 4], lhsT=bq[:, j:OQ:4], rhs=ident_b[:, 0:4], start=True, stop=True)
+        for z in range(NZ):
+            nc.tensor.matmul(
+                out=bc_ps[:, 16 + z : 17 + z], lhsT=bq[:, P * z : P * z + P], rhs=ident_b[:, 3:4], start=True, stop=True
+            )
+        bcol = keep.tile([P, 20], F32)
         nc.scalar.copy(out=bcol[:], in_=bc_ps[:])
-        nbcol = keep.tile([P, 4, NQ], F32)
+        nbcol = keep.tile([P, 20], F32)
         nc.vector.tensor_scalar_mul(out=nbcol[:], in0=bcol[:], scalar1=-1.0)
         xb = keep.tile([P, NB, NQ, 4 * S], F32)
         for q in range(NQ):
@@ -194,58 +218,91 @@ def tile_staticgraphmodule_w_kernel(tc, x, Wp_words, Wp_scales, b, out):
                 nc.vector.tensor_scalar_add(
                     out=xb[:, :, q, S * j : S * j + S],
                     in0=raw[:, :, q, S * j : S * j + S],
-                    scalar1=bcol[:, j, q : q + 1],
+                    scalar1=bcol[:, 4 * j + q : 4 * j + q + 1],
                 )
 
-        for g in range(2, GA):
-            for q in range(NQ):
-                mx_pass(g, q)
+        for g in range(2):
+            for z in range(1, NZ):
+                tile_pass(g, z)
+        for q in range(NQ):
+            quarter_pass(2, q)
+        for z in range(NZ):
+            tile_pass(2, z)
 
-        out_v = out.rearrange("n (q m j) h w -> q m n j (h w)", q=NQ, m=P, j=4)
+        res_ps = psum.tile([P, NZ, NB, S], F32, tag="bank4", name="res_ps")
+        for z in range(NZ):
+            for t in range(4):
+                nc.tensor.matmul(
+                    out=res_ps[:, z],
+                    lhsT=spread[:, t, P * z : P * z + P],
+                    rhs=raw[:, :, GX - 1, S * t : S * t + S],
+                    start=(t == 0),
+                    stop=(t == 3),
+                )
+        xbz = keep.tile([P, NZ, TOK], F32)
+        for z in range(NZ):
+            nc.vector.tensor_scalar_add(
+                out=xbz[:, z, :],
+                in0=res_ps[:, z].rearrange("p n s -> p (n s)"),
+                scalar1=bcol[:, 16 + z : 17 + z],
+            )
+
+        for q in range(NQ):
+            quarter_pass(3, q)
+        for z in range(NZ):
+            tile_pass(3, z)
+        for g in range(GW, GA):
+            for q in range(NQ):
+                quarter_pass(g, q)
+
+        out_v = out.rearrange("n (q m j) h w -> q m n j (h w)", q=4, m=P, j=4)
+        out_z = out.rearrange("n (a p) h w -> a p n (h w)", p=P)
         ys = [keep.tile([P, 4, P], F32, name="y%d" % q) for q in range(NQ)]
         os_ = [keep.tile([P, NB, 4, S], F32, name="o%d" % q) for q in range(NQ)]
 
         def last_passes(q):
             for g in range(GA, G):
-                mx_pass(g, q)
+                quarter_pass(g, q)
+            nc.scalar.copy(out=ys[q][:], in_=accs[q][:].rearrange("p (m j) -> p j m", j=4))
 
-        def copy_out(q, j0, j1):
-            nc.scalar.copy(out=ys[q][:, j0:j1, :], in_=accs[q][:].rearrange("p (m j) -> p j m", j=4)[:, j0:j1, :])
-
-        def turn_back(q, j0, j1, bank):
-            f_ps = psum.tile([P, NB, j1 - j0, S], F32, tag="bank%d" % bank, name="f_ps%d_%d" % (q, j0))
-            for j in range(j0, j1):
-                nc.tensor.transpose(f_ps[:, :, j - j0, :], ys[q][:, j, :], ident_f[:])
-            return f_ps
-
-        def relu_residual_store(q, j0, j1, f_ps):
-            for j in range(j0, j1):
+        def finish(q, bank):
+            f_ps = psum.tile([P, NB, 4, S], F32, tag="bank%d" % bank, name="f_ps%d" % q)
+            for j in range(4):
+                nc.tensor.transpose(f_ps[:, :, j, :], ys[q][:, j, :], ident_f[:])
+            for j in range(4):
                 nc.vector.scalar_tensor_tensor(
                     out=os_[q][:, :, j, :],
-                    in0=f_ps[:, :, j - j0, :],
-                    scalar=nbcol[:, j, q : q + 1],
+                    in0=f_ps[:, :, j, :],
+                    scalar=nbcol[:, 4 * j + q : 4 * j + q + 1],
                     in1=xb[:, :, q, S * j : S * j + S],
                     op0=ALU.max,
                     op1=ALU.add,
                 )
-            nc.sync.dma_start(out=out_v[q][:, :, j0:j1, :], in_=os_[q][:, :, j0:j1, :])
+            nc.sync.dma_start(out=out_v[q], in_=os_[q][:])
+
+        def tile_finish(z):
+            oz = keep.tile([P, NB, S], F32, name="oz%d" % z)
+            nc.vector.scalar_tensor_tensor(
+                out=oz[:].rearrange("p n s -> p (n s)"),
+                in0=z_ps[z][:],
+                scalar=nbcol[:, 16 + z : 17 + z],
+                in1=xbz[:, z, :],
+                op0=ALU.max,
+                op1=ALU.add,
+            )
+            nc.sync.dma_start(out=out_z[C // P - NZ + z], in_=oz[:])
 
         last_passes(0)
-        copy_out(0, 0, 4)
         last_passes(1)
-        copy_out(1, 0, 4)
-        f0 = turn_back(0, 0, 4, 4)
-        relu_residual_store(0, 0, 4, f0)
+        finish(0, 4)
         last_passes(2)
-        copy_out(2, 0, 4)
-        f1 = turn_back(1, 0, 4, 5)
-        relu_residual_store(1, 0, 4, f1)
-        last_passes(3)
-        copy_out(3, 0, 2)
-        copy_out(3, 2, 4)
-        f2 = turn_back(2, 0, 4, 6)
-        relu_residual_store(2, 0, 4, f2)
-        f3a = turn_back(3, 0, 2, 7)
-        f3b = turn_back(3, 2, 4, 4)
-        relu_residual_store(3, 0, 2, f3a)
-        relu_residual_store(3, 2, 4, f3b)
+        finish(1, 0)
+        for g in range(GW, GA):
+            for z in range(NZ):
+                tile_pass(g, z)
+        for z in range(NZ):
+            tile_pass(GA, z)
+        finish(2, 1)
+        for z in range(NZ):
+            tile_pass(GA + 1, z)
+            tile_finish(z)

@@ -300,9 +300,9 @@ def tile_staticgraphmodule_w_kernel(tc, x, Wp_words, Wp_scales, b, out):
         for g in range(GW, GA):
             for z in range(NZ):
                 tile_pass(g, z)
+        finish(2, 1)
         for z in range(NZ):
             tile_pass(GA, z)
-        finish(2, 1)
         for z in range(NZ):
             tile_pass(GA + 1, z)
             tile_finish(z)

@@ -24,7 +24,7 @@ NQ = 3
 OQ = 512
 CQ = NQ * OQ
 NZ = 4
-GW = 4
+GW = 3
 GA = 6
 
 FLOPS = 2 * TOK * 2 * C * C
@@ -80,14 +80,14 @@ def tile_staticgraphmodule_w_kernel(tc, x, Wp_words, Wp_scales, b, out):
         for g in range(3):
             load_words(g, g + 1, 0, C)
         load_scales(1)
-        load_words(3, 4, 0, C)
         for g in range(GW, GA):
             load_words(g, g + 1, 0, CQ)
         for q in range(NQ):
-            load_words(GA, G, OQ * q, OQ * (q + 1))
-        load_words(GW, GA, CQ, C)
-        load_words(GA, GA + 1, CQ, C)
-        load_words(GA + 1, G, CQ, C)
+            for g in range(GA, G):
+                load_words(g, g + 1, OQ * q, OQ * (q + 1))
+        load_words(GW, GW + 2, CQ, C)
+        for g in range(GW + 2, G):
+            load_words(g, g + 1, CQ, C)
 
         ident_b = keep.tile([P, P], BF16)
         ident_f = keep.tile([P, P], F32)
@@ -247,10 +247,6 @@ def tile_staticgraphmodule_w_kernel(tc, x, Wp_words, Wp_scales, b, out):
                 scalar1=bcol[:, 16 + z : 17 + z],
             )
 
-        for q in range(NQ):
-            quarter_pass(3, q)
-        for z in range(NZ):
-            tile_pass(3, z)
         for g in range(GW, GA):
             for q in range(NQ):
                 quarter_pass(g, q)
@@ -297,12 +293,13 @@ def tile_staticgraphmodule_w_kernel(tc, x, Wp_words, Wp_scales, b, out):
         finish(0, 4)
         last_passes(2)
         finish(1, 0)
-        for g in range(GW, GA):
+        for g in range(GW, GW + 2):
             for z in range(NZ):
                 tile_pass(g, z)
         finish(2, 1)
+        for g in range(GW + 2, G - 1):
+            for z in range(NZ):
+                tile_pass(g, z)
         for z in range(NZ):
-            tile_pass(GA, z)
-        for z in range(NZ):
-            tile_pass(GA + 1, z)
+            tile_pass(G - 1, z)
             tile_finish(z)

@@ -18,6 +18,7 @@ NB = 2
 C = 2048
 S = 64
 TOK = NB * S
+CN = C // P
 GX = 4
 G = 2 * GX
 NQ = 3
@@ -40,11 +41,8 @@ def tile_staticgraphmodule_w_kernel(tc, x, Wp_words, Wp_scales, b, out):
         bq = keep.tile([P, OQ], BF16)
         nc.vector.memset(bq[:].bitcast(I32), 0)
         nc.scalar.dma_start(out=bq[0:4, :], in_=b.rearrange("(q c) -> q c", q=4))
-        raw = keep.tile([P, NB, GX, 4 * S], BF16, align_bytes=64)
-        nc.sync.dma_start(
-            out=raw[:].rearrange("p n g f -> p (n g) f"),
-            in_=x.rearrange("n (g p t) h w -> p (n g) (t h w)", g=GX, p=P, t=4),
-        )
+        xn = keep.tile([P, NB, CN * S], BF16, align_bytes=64)
+        nc.sync.dma_start(out=xn[:], in_=x.rearrange("n (p c) h w -> p n (c h w)", p=P))
         one = keep.tile([P, 1], BF16)
         nc.vector.memset(one[:], 1.0)
         warm = keep.tile([P, 1], BF16)
@@ -111,19 +109,32 @@ def tile_staticgraphmodule_w_kernel(tc, x, Wp_words, Wp_scales, b, out):
         amat = keep.tile([P, P], BF16)
         nc.vector.tensor_scalar_mul(out=amat[:], in0=bflat, scalar1=0.125)
 
-        xt_sb = keep.tile([P, GX, 4, P], BF16)
-        for g in range(GX):
-            xt_ps = psum.tile([P, 4, P], BF16, tag="bank%d" % g, name="xt_ps%d" % g)
+        xt_sb = keep.tile([P, NB, 2, P, 4], BF16)
+        for v in range(2):
             for n in range(NB):
-                for u in range(2):
-                    nc.tensor.transpose(xt_ps[:, 2 * n + u, :], raw[:, n, g, P * u : P * u + P], ident_b[:])
-            nc.scalar.copy(out=xt_sb[:, g], in_=xt_ps[:])
+                xt_ps = psum.tile([P, 4, P], BF16, tag="bank%d" % (2 * v + n), name="xt_ps%d" % (2 * v + n))
+                for b4 in range(4):
+                    u = 2 * b4 + v
+                    nc.tensor.transpose(xt_ps[:, b4, :], xn[:, n, P * u : P * u + P], ident_b[:])
+                if n == 0:
+                    nc.scalar.copy(out=xt_sb[:, n, v], in_=xt_ps[:].rearrange("k b p -> k p b"))
+                else:
+                    nc.vector.tensor_copy(out=xt_sb[:, n, v], in_=xt_ps[:].rearrange("k b p -> k p b"))
+
+        def columns(g, n, v):
+            return xt_sb[:, n, v, 32 * g : 32 * g + 32, :].rearrange("k p b -> k (p b)")
+
         grouped_x = keep.tile([P, GX, NB, S, 4], BF16, align_bytes=64)
+        raw = keep.tile([P, GX, NB, 4, S], BF16, align_bytes=64)
         for g in range(GX):
-            nc.vector.tensor_copy(
-                out=grouped_x[:, g],
-                in_=raw[:, :, g, :].rearrange("p n (t s) -> p n s t", t=4),
-            )
+            x_ps = psum.tile([P, NB, 4, S], BF16, tag="bank%d" % g, name="x_ps%d" % g)
+            for n in range(NB):
+                for v in range(2):
+                    nc.tensor.transpose(
+                        x_ps[:, n, 2 * v : 2 * v + 2, :].rearrange("p e s -> p (e s)"), columns(g, n, v), ident_b[:]
+                    )
+            nc.vector.tensor_copy(out=grouped_x[:, g], in_=x_ps[:].rearrange("p n t s -> p n s t"))
+            nc.scalar.copy(out=raw[:, g], in_=x_ps[:])
         codes_x = keep.tile([P, GX * TOK], U32, align_bytes=64)
         scales_x = keep.tile([P, GX * TOK], U8, align_bytes=64)
         nc.vector.quantize_mx(
@@ -141,10 +152,10 @@ def tile_staticgraphmodule_w_kernel(tc, x, Wp_words, Wp_scales, b, out):
         for g in range(GX):
             m_ps = psum.tile([P, NB, 4, S], F32, tag="bank%d" % (4 + g), name="m_ps%d" % g)
             for n in range(NB):
-                for u in range(2):
+                for v in range(2):
                     nc.tensor.matmul(
-                        out=m_ps[:, n, 2 * u : 2 * u + 2, :].rearrange("p e s -> p (e s)"),
-                        lhsT=xt_sb[:, g, 2 * n + u, :],
+                        out=m_ps[:, n, 2 * v : 2 * v + 2, :].rearrange("p e s -> p (e s)"),
+                        lhsT=columns(g, n, v),
                         rhs=amat[:],
                         start=True,
                         stop=True,
@@ -217,7 +228,7 @@ def tile_staticgraphmodule_w_kernel(tc, x, Wp_words, Wp_scales, b, out):
             for j in range(4):
                 nc.vector.tensor_scalar_add(
                     out=xb[:, :, q, S * j : S * j + S],
-                    in0=raw[:, :, q, S * j : S * j + S],
+                    in0=raw[:, q, :, j, :],
                     scalar1=bcol[:, 4 * j + q : 4 * j + q + 1],
                 )
 
@@ -235,7 +246,7 @@ def tile_staticgraphmodule_w_kernel(tc, x, Wp_words, Wp_scales, b, out):
                 nc.tensor.matmul(
                     out=res_ps[:, z],
                     lhsT=spread[:, t, P * z : P * z + P],
-                    rhs=raw[:, :, GX - 1, S * t : S * t + S],
+                    rhs=raw[:, GX - 1, :, t, :],
                     start=(t == 0),
                     stop=(t == 3),
                 )

@@ -26,7 +26,7 @@ OQ = 512
 CQ = NQ * OQ
 NZ = 4
 GW = 3
-GA = 6
+GA = 7
 
 FLOPS = 2 * TOK * 2 * C * C
 
@@ -92,6 +92,11 @@ def tile_staticgraphmodule_w_kernel(tc, x, Wp_words, Wp_scales, b, out):
         make_identity(nc, ident_b[:])
         make_identity(nc, ident_f[:])
 
+        spread = keep.tile([P, 4, OQ], BF16)
+        nc.gpsimd.memset(spread[:].bitcast(I32), 0)
+        for t in range(4):
+            nc.gpsimd.tensor_copy(out=spread[:, t, t:OQ:4], in_=ident_b[:])
+
         hmat = keep.tile([P, 16, 8], F32)
         i3 = ident_f[:].rearrange("p (a j) -> p a j", j=8)
         nc.vector.tensor_tensor(out=hmat[:, :, 1:8], in0=i3[:, :, 1:8], in1=i3[:, :, 0:7], op=ALU.add)
@@ -124,54 +129,47 @@ def tile_staticgraphmodule_w_kernel(tc, x, Wp_words, Wp_scales, b, out):
         def columns(g, n, v):
             return xt_sb[:, n, v, 32 * g : 32 * g + 32, :].rearrange("k p b -> k (p b)")
 
-        grouped_x = keep.tile([P, GX, NB, S, 4], BF16, align_bytes=64)
-        raw = keep.tile([P, GX, NB, 4, S], BF16, align_bytes=64)
-        for g in range(GX):
-            x_ps = psum.tile([P, NB, 4, S], BF16, tag="bank%d" % g, name="x_ps%d" % g)
+        x_ps = [psum.tile([P, NB, 4, S], BF16, tag="bank%d" % g, name="x_ps%d" % g) for g in range(GX)]
+        m_ps = [psum.tile([P, NB, 4, S], F32, tag="bank%d" % (4 + g), name="m_ps%d" % g) for g in range(GX)]
+        for v in range(2):
             for n in range(NB):
-                for v in range(2):
+                for g in range(GX):
                     nc.tensor.transpose(
-                        x_ps[:, n, 2 * v : 2 * v + 2, :].rearrange("p e s -> p (e s)"), columns(g, n, v), ident_b[:]
+                        x_ps[g][:, n, 2 * v : 2 * v + 2, :].rearrange("p e s -> p (e s)"), columns(g, n, v), ident_b[:]
                     )
-            nc.vector.tensor_copy(out=grouped_x[:, g], in_=x_ps[:].rearrange("p n t s -> p n s t"))
-            nc.scalar.copy(out=raw[:, g], in_=x_ps[:])
-        codes_x = keep.tile([P, GX * TOK], U32, align_bytes=64)
-        scales_x = keep.tile([P, GX * TOK], U8, align_bytes=64)
-        nc.vector.quantize_mx(
-            out=codes_x[:].bitcast(FP8X4),
-            scales=scales_x[:],
-            in_=grouped_x[:].rearrange("p g n s t -> p (g n s t)"),
-        )
-
-        spread = keep.tile([P, 4, OQ], BF16)
-        nc.vector.memset(spread[:].bitcast(I32), 0)
-        for t in range(4):
-            nc.vector.tensor_copy(out=spread[:, t, t:OQ:4], in_=ident_b[:])
-
-        grouped_m = keep.tile([P, GX, NB, S, 4], BF16, align_bytes=64)
         for g in range(GX):
-            m_ps = psum.tile([P, NB, 4, S], F32, tag="bank%d" % (4 + g), name="m_ps%d" % g)
-            for n in range(NB):
-                for v in range(2):
+            for v in range(2):
+                for n in range(NB):
                     nc.tensor.matmul(
-                        out=m_ps[:, n, 2 * v : 2 * v + 2, :].rearrange("p e s -> p (e s)"),
+                        out=m_ps[g][:, n, 2 * v : 2 * v + 2, :].rearrange("p e s -> p (e s)"),
                         lhsT=columns(g, n, v),
                         rhs=amat[:],
                         start=True,
                         stop=True,
                     )
-            src = m_ps[:].rearrange("p n t s -> p n s t")
-            if g % 2 == 0:
-                nc.vector.tensor_copy(out=grouped_m[:, g], in_=src)
-            else:
-                nc.scalar.copy(out=grouped_m[:, g], in_=src)
-        codes_m = keep.tile([P, GX * TOK], U32, align_bytes=64)
-        scales_m = keep.tile([P, GX * TOK], U8, align_bytes=64)
-        nc.vector.quantize_mx(
-            out=codes_m[:].bitcast(FP8X4),
-            scales=scales_m[:],
-            in_=grouped_m[:].rearrange("p g n s t -> p (g n s t)"),
-        )
+
+        HALF = GX // 2 * TOK
+
+        def quantised(name, sources):
+            grouped = keep.tile([P, GX, NB, S, 4], BF16, align_bytes=64, name="grouped_" + name)
+            codes = keep.tile([P, GX * TOK], U32, align_bytes=64, name="codes_" + name)
+            scales = keep.tile([P, GX * TOK], U8, align_bytes=64, name="scales_" + name)
+            for h in range(2):
+                for g in (2 * h, 2 * h + 1):
+                    src = sources[g][:].rearrange("p n t s -> p n s t")
+                    if g % 2 == 0:
+                        nc.vector.tensor_copy(out=grouped[:, g], in_=src)
+                    else:
+                        nc.scalar.copy(out=grouped[:, g], in_=src)
+                nc.vector.quantize_mx(
+                    out=codes[:, HALF * h : HALF * h + HALF].bitcast(FP8X4),
+                    scales=scales[:, HALF * h : HALF * h + HALF],
+                    in_=grouped[:, 2 * h : 2 * h + 2].rearrange("p g n s t -> p (g n s t)"),
+                )
+            return grouped, codes, scales
+
+        grouped_x, codes_x, scales_x = quantised("x", x_ps)
+        grouped_m, codes_m, scales_m = quantised("m", m_ps)
 
         accs = [psum.tile([P, OQ], F32, tag="bank%d" % q, name="acc%d" % q) for q in range(NQ)]
         Z_BANKS = [3, 5, 6, 7]
@@ -207,7 +205,7 @@ def tile_staticgraphmodule_w_kernel(tc, x, Wp_words, Wp_scales, b, out):
                 stop=(g == G - 1),
             )
 
-        for g in range(2):
+        for g in range(3):
             for q in range(NQ):
                 quarter_pass(g, q)
             tile_pass(g, 0)
@@ -228,17 +226,13 @@ def tile_staticgraphmodule_w_kernel(tc, x, Wp_words, Wp_scales, b, out):
             for j in range(4):
                 nc.vector.tensor_scalar_add(
                     out=xb[:, :, q, S * j : S * j + S],
-                    in0=raw[:, q, :, j, :],
+                    in0=grouped_x[:, q, :, :, j],
                     scalar1=bcol[:, 4 * j + q : 4 * j + q + 1],
                 )
 
-        for g in range(2):
+        for g in range(3):
             for z in range(1, NZ):
                 tile_pass(g, z)
-        for q in range(NQ):
-            quarter_pass(2, q)
-        for z in range(NZ):
-            tile_pass(2, z)
 
         res_ps = psum.tile([P, NZ, NB, S], F32, tag="bank4", name="res_ps")
         for z in range(NZ):
@@ -246,7 +240,7 @@ def tile_staticgraphmodule_w_kernel(tc, x, Wp_words, Wp_scales, b, out):
                 nc.tensor.matmul(
                     out=res_ps[:, z],
                     lhsT=spread[:, t, P * z : P * z + P],
-                    rhs=raw[:, GX - 1, :, t, :],
+                    rhs=grouped_x[:, GX - 1, :, :, t],
                     start=(t == 0),
                     stop=(t == 3),
                 )
@@ -270,7 +264,11 @@ def tile_staticgraphmodule_w_kernel(tc, x, Wp_words, Wp_scales, b, out):
         def last_passes(q):
             for g in range(GA, G):
                 quarter_pass(g, q)
-            nc.scalar.copy(out=ys[q][:], in_=accs[q][:].rearrange("p (m j) -> p j m", j=4))
+            src = accs[q][:].rearrange("p (m j) -> p j m", j=4)
+            if q == 1:
+                nc.vector.tensor_copy(out=ys[q][:], in_=src)
+            else:
+                nc.scalar.copy(out=ys[q][:], in_=src)
 
         def finish(q, bank):
             f_ps = psum.tile([P, NB, 4, S], F32, tag="bank%d" % bank, name="f_ps%d" % q)
@@ -299,10 +297,9 @@ def tile_staticgraphmodule_w_kernel(tc, x, Wp_words, Wp_scales, b, out):
             )
             nc.sync.dma_start(out=out_z[C // P - NZ + z], in_=oz[:])
 
-        last_passes(0)
-        last_passes(1)
+        for q in range(NQ):
+            last_passes(q)
         finish(0, 4)
-        last_passes(2)
         finish(1, 0)
         for g in range(GW, GW + 2):
             for z in range(NZ):

@@ -252,9 +252,11 @@ def tile_staticgraphmodule_w_kernel(tc, x, Wp_words, Wp_scales, b, out):
                 scalar1=bcol[:, 16 + z : 17 + z],
             )
 
-        for g in range(GW, GA):
+        for g in range(GW, GA - 1):
             for q in range(NQ):
                 quarter_pass(g, q)
+        quarter_pass(GA - 1, 0)
+        quarter_pass(GA - 1, 1)
 
         out_v = out.rearrange("n (q m j) h w -> q m n j (h w)", q=4, m=P, j=4)
         out_z = out.rearrange("n (a p) h w -> a p n (h w)", p=P)
@@ -297,15 +299,14 @@ def tile_staticgraphmodule_w_kernel(tc, x, Wp_words, Wp_scales, b, out):
             )
             nc.sync.dma_start(out=out_z[C // P - NZ + z], in_=oz[:])
 
-        for q in range(NQ):
-            last_passes(q)
+        last_passes(0)
+        quarter_pass(GA - 1, 2)
+        last_passes(1)
+        last_passes(2)
         finish(0, 4)
         finish(1, 0)
-        for g in range(GW, GW + 2):
-            for z in range(NZ):
-                tile_pass(g, z)
         finish(2, 1)
-        for g in range(GW + 2, G - 1):
+        for g in range(GW, G - 1):
             for z in range(NZ):
                 tile_pass(g, z)
         for z in range(NZ):

@@ -25,7 +25,7 @@ NQ = 3
 OQ = 512
 CQ = NQ * OQ
 NZ = 4
-GW = 3
+GW = 2
 GA = 7
 
 FLOPS = 2 * TOK * 2 * C * C
@@ -75,10 +75,11 @@ def tile_staticgraphmodule_w_kernel(tc, x, Wp_words, Wp_scales, b, out):
         for a in range(2):
             nc.vector.memset(planes[a][:].bitcast(I32), 0)
         load_scales(0)
-        for g in range(3):
+        for g in range(GW):
             load_words(g, g + 1, 0, C)
+        load_words(GW, GW + 1, 0, CQ)
         load_scales(1)
-        for g in range(GW, GA):
+        for g in range(GW + 1, GA):
             load_words(g, g + 1, 0, CQ)
         for q in range(NQ):
             for g in range(GA, G):
@@ -205,10 +206,12 @@ def tile_staticgraphmodule_w_kernel(tc, x, Wp_words, Wp_scales, b, out):
                 stop=(g == G - 1),
             )
 
-        for g in range(3):
+        for g in range(GW):
             for q in range(NQ):
                 quarter_pass(g, q)
             tile_pass(g, 0)
+        for q in range(NQ):
+            quarter_pass(GW, q)
 
         bc_ps = psum.tile([P, 20], F32, tag="bank4", name="bc_ps")
         for j in range(4):
@@ -230,7 +233,7 @@ def tile_staticgraphmodule_w_kernel(tc, x, Wp_words, Wp_scales, b, out):
                     scalar1=bcol[:, 4 * j + q : 4 * j + q + 1],
                 )
 
-        for g in range(3):
+        for g in range(GW):
             for z in range(1, NZ):
                 tile_pass(g, z)
 
@@ -252,7 +255,7 @@ def tile_staticgraphmodule_w_kernel(tc, x, Wp_words, Wp_scales, b, out):
                 scalar1=bcol[:, 16 + z : 17 + z],
             )
 
-        for g in range(GW, GA - 1):
+        for g in range(GW + 1, GA - 1):
             for q in range(NQ):
                 quarter_pass(g, q)
         quarter_pass(GA - 1, 0)

from contextlib import ExitStack

import concourse.bass as bass
import concourse.mybir as mybir
import concourse.tile as tile
from concourse.masks import make_identity

BF16 = mybir.dt.bfloat16
F32 = mybir.dt.float32
I32 = mybir.dt.int32
U8 = mybir.dt.uint8
U32 = mybir.dt.uint32
FP8X4 = mybir.dt.float8_e4m3fn_x4
ALU = mybir.AluOpType

P = 128
NB = 2
C = 2048
S = 64
TOK = NB * S
CN = C // P
GX = 4
G = 2 * GX
NQ = 3
OQ = 512
CQ = NQ * OQ
NZ = 4
GW = 2
GA = 7

FLOPS = 2 * TOK * 2 * C * C


def tile_staticgraphmodule_w_kernel(tc, x, Wp_words, Wp_scales, b, out):
    nc = tc.nc
    with ExitStack() as ctx:
        keep = ctx.enter_context(tc.tile_pool(name="keep", bufs=1))
        psum = ctx.enter_context(tc.psum_pool(name="psum", bufs=1))
        ctx.enter_context(tc.manual_schedule())

        bq = keep.tile([P, OQ], BF16)
        nc.vector.memset(bq[:].bitcast(I32), 0)
        nc.scalar.dma_start(out=bq[0:4, :], in_=b.rearrange("(q c) -> q c", q=4))
        xn = keep.tile([P, NB, CN * S], BF16, align_bytes=64)
        nc.sync.dma_start(out=xn[:], in_=x.rearrange("n (p c) h w -> p n (c h w)", p=P))
        one = keep.tile([P, 1], BF16)
        nc.vector.memset(one[:], 1.0)
        warm = keep.tile([P, 1], BF16)
        nc.scalar.copy(out=warm[:], in_=one[:])
        planes = [keep.tile([P, C], U8, align_bytes=64, name="plane%d" % a) for a in range(2)]

        def load_scales(a):
            for q in range(4):
                nc.sync.dma_start(
                    out=planes[a][32 * q : 32 * q + 16, :].bitcast(I32),
                    in_=Wp_scales[4 * a : 4 * a + 4, 4 * q : 4 * q + 4, :].bitcast(I32),
                )

        words = {}

        def load_words(g0, g1, c0, c1):
            wt = keep.tile([P, g1 - g0, 4 * (c1 - c0)], U8, align_bytes=64, name="w%d_%d" % (g0, c0))
            nc.sync.dma_start(
                out=wt[:].bitcast(I32),
                in_=Wp_words[g0:g1, :, c0:c1, :].rearrange("g p n t -> p g (n t)").bitcast(I32),
            )
            for g in range(g0, g1):
                for c in range(c0, c1, P):
                    if c < CQ:
                        if c % OQ == 0:
                            words[(g, c)] = wt[:, g - g0, 4 * (c - c0) : 4 * (c - c0 + OQ)]
                    else:
                        words[(g, c)] = wt[:, g - g0, 4 * (c - c0) : 4 * (c - c0 + P)]

        for a in range(2):
            nc.vector.memset(planes[a][:].bitcast(I32), 0)
        load_scales(0)
        for g in range(GW):
            load_words(g, g + 1, 0, C)
        load_words(GW, GW + 1, 0, CQ)
        load_scales(1)
        for g in range(GW + 1, GA):
            load_words(g, g + 1, 0, CQ)
        for q in range(NQ):
            for g in range(GA, G):
                load_words(g, g + 1, OQ * q, OQ * (q + 1))
        load_words(GW, GW + 2, CQ, C)
        for g in range(GW + 2, G):
            load_words(g, g + 1, CQ, C)

        ident_b = keep.tile([P, P], BF16)
        ident_f = keep.tile([P, P], F32)
        make_identity(nc, ident_b[:])
        make_identity(nc, ident_f[:])

        spread = keep.tile([P, 4, OQ], BF16)
        nc.gpsimd.memset(spread[:].bitcast(I32), 0)
        for t in range(4):
            nc.gpsimd.tensor_copy(out=spread[:, t, t:OQ:4], in_=ident_b[:])

        hmat = keep.tile([P, 16, 8], F32)
        i3 = ident_f[:].rearrange("p (a j) -> p a j", j=8)
        nc.vector.tensor_tensor(out=hmat[:, :, 1:8], in0=i3[:, :, 1:8], in1=i3[:, :, 0:7], op=ALU.add)
        nc.vector.tensor_scalar_mul(out=hmat[:, :, 0:1], in0=i3[:, :, 0:1], scalar1=2.0)
        nc.vector.tensor_tensor(out=hmat[:, :, 0:7], in0=hmat[:, :, 0:7], in1=i3[:, :, 1:8], op=ALU.add)
        nc.vector.tensor_tensor(out=hmat[:, :, 7:8], in0=hmat[:, :, 7:8], in1=i3[:, :, 7:8], op=ALU.add)
        bmat = keep.tile([P, 2, 8, 8], F32)
        h4 = hmat[:].rearrange("p (e i) j -> p e i j", e=2)
        nc.vector.tensor_tensor(out=bmat[:, :, 1:8, :], in0=h4[:, :, 1:8, :], in1=h4[:, :, 0:7, :], op=ALU.add)
        nc.vector.tensor_scalar_mul(out=bmat[:, :, 0:1, :], in0=h4[:, :, 0:1, :], scalar1=2.0)
        nc.vector.tensor_tensor(out=bmat[:, :, 0:7, :], in0=bmat[:, :, 0:7, :], in1=h4[:, :, 1:8, :], op=ALU.add)
        nc.vector.tensor_tensor(out=bmat[:, :, 7:8, :], in0=bmat[:, :, 7:8, :], in1=h4[:, :, 7:8, :], op=ALU.add)
        bflat = bmat[:].rearrange("p e i j -> p (e i j)")
        nc.vector.tensor_tensor(out=bflat, in0=bflat, in1=ident_f[:], op=ALU.subtract)
        amat = keep.tile([P, P], BF16)
        nc.vector.tensor_scalar_mul(out=amat[:], in0=bflat, scalar1=0.125)

        xt_sb = keep.tile([P, NB, 2, P, 4], BF16)
        for v in range(2):
            for n in range(NB):
                xt_ps = psum.tile([P, 4, P], BF16, tag="bank%d" % (2 * v + n), name="xt_ps%d" % (2 * v + n))
                for b4 in range(4):
                    u = 2 * b4 + v
                    nc.tensor.transpose(xt_ps[:, b4, :], xn[:, n, P * u : P * u + P], ident_b[:])
                if n == 0:
                    nc.scalar.copy(out=xt_sb[:, n, v], in_=xt_ps[:].rearrange("k b p -> k p b"))
                else:
                    nc.vector.tensor_copy(out=xt_sb[:, n, v], in_=xt_ps[:].rearrange("k b p -> k p b"))

        def columns(g, n, v):
            return xt_sb[:, n, v, 32 * g : 32 * g + 32, :].rearrange("k p b -> k (p b)")

        x_ps = [psum.tile([P, NB, 4, S], BF16, tag="bank%d" % g, name="x_ps%d" % g) for g in range(GX)]
        m_ps = [psum.tile([P, NB, 4, S], F32, tag="bank%d" % (4 + g), name="m_ps%d" % g) for g in range(GX)]
        for v in range(2):
            for n in range(NB):
                for g in range(GX):
                    nc.tensor.transpose(
                        x_ps[g][:, n, 2 * v : 2 * v + 2, :].rearrange("p e s -> p (e s)"), columns(g, n, v), ident_b[:]
                    )
        for g in range(GX):
            for v in range(2):
                for n in range(NB):
                    nc.tensor.matmul(
                        out=m_ps[g][:, n, 2 * v : 2 * v + 2, :].rearrange("p e s -> p (e s)"),
                        lhsT=columns(g, n, v),
                        rhs=amat[:],
                        start=True,
                        stop=True,
                    )

        HALF = GX // 2 * TOK

        def quantised(name, sources):
            grouped = keep.tile([P, GX, NB, S, 4], BF16, align_bytes=64, name="grouped_" + name)
            codes = keep.tile([P, GX * TOK], U32, align_bytes=64, name="codes_" + name)
            scales = keep.tile([P, GX * TOK], U8, align_bytes=64, name="scales_" + name)
            for h in range(2):
                for g in (2 * h, 2 * h + 1):
                    src = sources[g][:].rearrange("p n t s -> p n s t")
                    if g % 2 == 0:
                        nc.vector.tensor_copy(out=grouped[:, g], in_=src)
                    else:
                        nc.scalar.copy(out=grouped[:, g], in_=src)
                nc.vector.quantize_mx(
                    out=codes[:, HALF * h : HALF * h + HALF].bitcast(FP8X4),
                    scales=scales[:, HALF * h : HALF * h + HALF],
                    in_=grouped[:, 2 * h : 2 * h + 2].rearrange("p g n s t -> p (g n s t)"),
                )
            return grouped, codes, scales

        grouped_x, codes_x, scales_x = quantised("x", x_ps)
        grouped_m, codes_m, scales_m = quantised("m", m_ps)

        accs = [psum.tile([P, OQ], F32, tag="bank%d" % q, name="acc%d" % q) for q in range(NQ)]
        Z_BANKS = [3, 5, 6, 7]
        z_ps = [psum.tile([P, TOK], F32, tag="bank%d" % Z_BANKS[z], name="z_ps%d" % z) for z in range(NZ)]

        def operand(g):
            codes, scl = (codes_x, scales_x) if g < GX else (codes_m, scales_m)
            cols = slice(TOK * (g % GX), TOK * (g % GX) + TOK)
            return codes[:, cols].bitcast(FP8X4), scl[:, cols]

        def quarter_pass(g, q):
            act_codes, act_scales = operand(g)
            nc.tensor.matmul_mx(
                out=accs[q][:],
                lhsT=act_codes,
                lhsT_scale=act_scales,
                rhs=words[(g, OQ * q)].bitcast(FP8X4),
                rhs_scale=planes[g // 4][4 * (g % 4) : P, OQ * q : OQ * (q + 1)],
                start=(g == 0),
                stop=(g == G - 1),
            )

        def tile_pass(g, z):
            act_codes, act_scales = operand(g)
            c0 = CQ + P * z
            nc.tensor.matmul_mx(
                out=z_ps[z][:],
                lhsT=words[(g, c0)].bitcast(FP8X4),
                lhsT_scale=planes[g // 4][4 * (g % 4) : P, c0 : c0 + P],
                rhs=act_codes,
                rhs_scale=act_scales,
                start=(g == 0),
                stop=(g == G - 1),
            )

        for g in range(GW):
            for q in range(NQ):
                quarter_pass(g, q)
            tile_pass(g, 0)
        for q in range(NQ):
            quarter_pass(GW, q)

        bc_ps = psum.tile([P, 20], F32, tag="bank4", name="bc_ps")
        for j in range(4):
            nc.tensor.matmul(out=bc_ps[:, 4 * j : 4 * j + 4], lhsT=bq[:, j:OQ:4], rhs=ident_b[:, 0:4], start=True, stop=True)
        for z in range(NZ):
            nc.tensor.matmul(
                out=bc_ps[:, 16 + z : 17 + z], lhsT=bq[:, P * z : P * z + P], rhs=ident_b[:, 3:4], start=True, stop=True
            )
        bcol = keep.tile([P, 20], F32)
        nc.scalar.copy(out=bcol[:], in_=bc_ps[:])
        nbcol = keep.tile([P, 20], F32)
        nc.vector.tensor_scalar_mul(out=nbcol[:], in0=bcol[:], scalar1=-1.0)
        xb = keep.tile([P, NB, NQ, 4 * S], F32)
        for q in range(NQ):
            for j in range(4):
                nc.vector.tensor_scalar_add(
                    out=xb[:, :, q, S * j : S * j + S],
                    in0=grouped_x[:, q, :, :, j],
                    scalar1=bcol[:, 4 * j + q : 4 * j + q + 1],
                )

        for g in range(GW):
            for z in range(1, NZ):
                tile_pass(g, z)

        res_ps = psum.tile([P, NZ, NB, S], F32, tag="bank4", name="res_ps")
        for z in range(NZ):
            for t in range(4):
                nc.tensor.matmul(
                    out=res_ps[:, z],
                    lhsT=spread[:, t, P * z : P * z + P],
                    rhs=grouped_x[:, GX - 1, :, :, t],
                    start=(t == 0),
                    stop=(t == 3),
                )
        xbz = keep.tile([P, NZ, TOK], F32)
        for z in range(NZ):
            nc.vector.tensor_scalar_add(
                out=xbz[:, z, :],
                in0=res_ps[:, z].rearrange("p n s -> p (n s)"),
                scalar1=bcol[:, 16 + z : 17 + z],
            )

        for g in range(GW + 1, GA - 1):
            for q in range(NQ):
                quarter_pass(g, q)
        quarter_pass(GA - 1, 0)
        quarter_pass(GA - 1, 1)

        out_v = out.rearrange("n (q m j) h w -> q m n j (h w)", q=4, m=P, j=4)
        out_z = out.rearrange("n (a p) h w -> a p n (h w)", p=P)
        ys = [keep.tile([P, 4, P], F32, name="y%d" % q) for q in range(NQ)]
        os_ = [keep.tile([P, NB, 4, S], F32, name="o%d" % q) for q in range(NQ)]

        def last_passes(q):
            for g in range(GA, G):
                quarter_pass(g, q)
            src = accs[q][:].rearrange("p (m j) -> p j m", j=4)
            if q == 1:
                nc.vector.tensor_copy(out=ys[q][:], in_=src)
            else:
                nc.scalar.copy(out=ys[q][:], in_=src)

        def finish(q, bank):
            f_ps = psum.tile([P, NB, 4, S], F32, tag="bank%d" % bank, name="f_ps%d" % q)
            for j in range(4):
                nc.tensor.transpose(f_ps[:, :, j, :], ys[q][:, j, :], ident_f[:])
            for j in range(4):
                nc.vector.scalar_tensor_tensor(
                    out=os_[q][:, :, j, :],
                    in0=f_ps[:, :, j, :],
                    scalar=nbcol[:, 4 * j + q : 4 * j + q + 1],
                    in1=xb[:, :, q, S * j : S * j + S],
                    op0=ALU.max,
                    op1=ALU.add,
                )
            nc.sync.dma_start(out=out_v[q], in_=os_[q][:])

        def tile_finish(z):
            oz = keep.tile([P, NB, S], F32, name="oz%d" % z)
            nc.vector.scalar_tensor_tensor(
                out=oz[:].rearrange("p n s -> p (n s)"),
                in0=z_ps[z][:],
                scalar=nbcol[:, 16 + z : 17 + z],
                in1=xbz[:, z, :],
                op0=ALU.max,
                op1=ALU.add,
            )
            nc.sync.dma_start(out=out_z[C // P - NZ + z], in_=oz[:])

        last_passes(0)
        quarter_pass(GA - 1, 2)
        last_passes(1)
        last_passes(2)
        finish(0, 4)
        finish(1, 0)
        finish(2, 1)
        for g in range(GW, G - 1):
            for z in range(NZ):
                tile_pass(g, z)
        for z in range(NZ):
            tile_pass(G - 1, z)
            tile_finish(z)
